import numpy as np
import ml_dtypes


def mxq(x, axis, fmt="e4m3"):
    dtype, down = {"e4m3": (ml_dtypes.float8_e4m3fn, 7), "e5m2": (ml_dtypes.float8_e5m2, 14)}[fmt]
    v = np.moveaxis(np.asarray(x, np.float32).astype(ml_dtypes.bfloat16).astype(np.float64), axis, -1)
    blocks = v.reshape(v.shape[:-1] + (-1, 32))
    amax = np.abs(blocks).max(-1, keepdims=True)
    byte = np.maximum(np.where(amax > 0, np.frexp(amax)[1] - 1 + 127, 0) - down, 1)
    scale = np.exp2(byte - 127.0)
    codes = (blocks / scale).astype(np.float32).astype(dtype).astype(np.float64)
    return np.moveaxis((codes * scale).reshape(v.shape), -1, axis)


WIDE = False


def mx_kscale(k):
    if not WIDE:
        return np.ones(k)
    levels = np.array([10, -10, 5, -5, 0])
    if k % 512:
        return np.exp2(np.random.permutation(np.resize(levels, k // 32))).repeat(32)
    a = np.empty((k // 512, 16))
    for p in range(k // 512):
        a[p, :8] = np.random.permutation(np.resize(levels, 8))
        for g in range(8):
            far = levels[np.abs(levels - a[p, g]) >= 10]
            a[p, g + 8] = far[np.random.randint(len(far))]
    return np.exp2(a.ravel()).repeat(32)


BF16 = ml_dtypes.bfloat16


def bf(x):
    return np.asarray(x, np.float32).astype(BF16)


def f64(x):
    return np.asarray(x).astype(np.float64)


B, CB, CD, H, W = 4, 4, 512, 16, 16
C = CB * CD
T = B * H * W


def erf(a):
    a = np.clip(a, -6.0, 6.0)
    a2 = 2.0 * a * a
    term = a.copy()
    tot = a.copy()
    for n in range(1, 151):
        term = term * a2 / (2 * n + 1)
        tot = tot + term
    return 2.0 / np.sqrt(np.pi) * np.exp(-a * a) * tot


def gelu_erf(v):
    return 0.5 * v * (1.0 + erf(v / np.sqrt(2.0)))


def dgelu_erf(v):
    return 0.5 * (1.0 + erf(v / np.sqrt(2.0))) + v * np.exp(-0.5 * v * v) / np.sqrt(2.0 * np.pi)


def to_blocks(v):
    return v.transpose(1, 0, 2, 3).reshape(CB, CD, T)


def from_blocks(v):
    return v.reshape(C, B, H, W).transpose(1, 0, 2, 3)


def preact(x, wc):
    xb = to_blocks(x)
    mix = wc.transpose(0, 2, 1) @ xb
    return x + from_blocks(mix)


def setup_inputs():
    s = mx_kscale(T).reshape(B, 1, H, W)
    u = mx_kscale(CD)
    u = u / u.max()
    uc = np.tile(u, CB).reshape(1, C, 1, 1)
    x0 = bf(np.random.standard_normal((B, C, H, W)))
    wc0 = bf(np.random.standard_normal((CB, CD, CD)) / np.sqrt(CD))
    g = bf(np.random.standard_normal((B, C, H, W)) * np.exp2(np.random.randint(-6, 1, (B, 1, H, W))) / s * uc)
    z = preact(f64(x0), f64(wc0))
    return {"x": bf(f64(x0) * s), "wc": bf(f64(wc0) / u[None, None, :]), "z": np.asarray(z, np.float32), "grad_out": g}


def reference(x, wc, z, grad_out):
    dz = f64(grad_out) * dgelu_erf(f64(z))
    xb = to_blocks(f64(x))
    db = to_blocks(dz)
    mixback = mxq(f64(wc), 2, "e4m3") @ mxq(db, 1, "e5m2")
    dx = dz + from_blocks(mixback)
    dwc = mxq(xb, 2, "e4m3") @ mxq(db, 2, "e5m2").transpose(0, 2, 1)
    return dx, dwc

@@ -1,0 +1,275 @@
+from contextlib import ExitStack
+
+import concourse.mybir as mybir
+from concourse.masks import make_identity
+
+F32 = mybir.dt.float32
+BF16 = mybir.dt.bfloat16
+U32 = mybir.dt.uint32
+U8 = mybir.dt.uint8
+E4 = mybir.dt.float8_e4m3fn_x4
+E5 = mybir.dt.float8_e5m2_x4
+AF = mybir.ActivationFunctionType
+ALU = mybir.AluOpType
+
+P = 128
+CB = 4
+CD = 512
+UNITS = 8
+FLOPS = 2 * 2 * CB * CD * CD * 1024
+INV_SQRT_2PI = 0.3989422804014327
+
+GP_ON_POOL = False
+
+
+def tile_spectralchannelmixing_v_kernel(tc, x, wc, z, grad_out, out_0, out_1):
+    nc = tc.nc
+    with ExitStack() as ctx:
+        ctx.enter_context(tc.manual_schedule())
+        const = ctx.enter_context(tc.tile_pool(name="const", bufs=1))
+        sb = ctx.enter_context(tc.tile_pool(name="sb", bufs=2))
+        psum = ctx.enter_context(tc.psum_pool(name="psum", bufs=2))
+
+        zt, gt, at, st, lt = {}, {}, {}, {}, {}
+        raw, grp, dzb, gk = {}, {}, {}, {}
+        xq, xs, wq, ws, kq, ks, tq, ts = {}, {}, {}, {}, {}, {}, {}, {}
+        banks, o0, o1 = {}, {}, {}
+
+        def unit_view(t, u):
+            i, g = divmod(u, 2)
+            return t[2 * g : 2 * g + 2, CD * i : CD * (i + 1)].rearrange("b (p j) h w -> p b (j h w)", j=4)
+
+        def flat(t):
+            return t[:].rearrange("p b j t -> p (b j t)")
+
+        def load_z(u):
+            zt[u] = sb.tile([P, 2, 4, 256], F32, name="z%d" % u, tag="z", bufs=4)
+            nc.sync.dma_start(out=zt[u][:].rearrange("p b j t -> p b (j t)"), in_=unit_view(z, u))
+
+        def load_g(u):
+            gt[u] = sb.tile([P, 2, 4, 256], BF16, name="g%d" % u, tag="g", bufs=3)
+            nc.sync.dma_start(out=gt[u][:].rearrange("p b j t -> p b (j t)"), in_=unit_view(grad_out, u))
+
+        RAW = [("w", 0), ("x", 0), ("x", 1), ("w", 1), ("x", 2), ("x", 3), ("w", 2), ("x", 4), ("x", 5), ("w", 3), ("x", 6), ("x", 7)]
+
+        def load_raw(r):
+            kind, n = RAW[r]
+            raw[r] = sb.tile([P, 4, 512], BF16, name="raw%d" % r, tag="raw", bufs=3)
+            if kind == "w":
+                nc.sync.dma_start(out=raw[r][:], in_=wc[n].rearrange("(m t) k -> m t k", t=4))
+            else:
+                i, g = divmod(n, 2)
+                for bb in range(2):
+                    nc.sync.dma_start(
+                        out=raw[r][:, :, 256 * bb : 256 * (bb + 1)],
+                        in_=x[2 * g + bb, CD * i : CD * (i + 1)].rearrange("(p j) h w -> p j (h w)", j=4),
+                    )
+
+        def fill_bank(key, src, h):
+            words = src[:].rearrange("p j t -> p (j t)").bitcast(F32)
+            banks[key] = psum.tile([P, 512], F32, name="tp_%s" % key, tag="tp", bufs=2)
+            for jj in range(2):
+                for w in range(2):
+                    j = 2 * h + jj
+                    c = 128 * (2 * jj + w)
+                    nc.tensor.transpose(banks[key][:, c : c + 128], words[:, 256 * j + w : 256 * (j + 1) : 2], ident[:])
+
+        def empty_bank(eng_copy, key, dst, h):
+            out = dst[:].bitcast(F32)[:, 512 * h : 512 * (h + 1)].rearrange("q (j m w) -> q j m w", j=2, w=2)
+            eng_copy(out=out, in_=banks[key][:].rearrange("q (j w m) -> q j m w", j=2, w=2))
+
+        def new_grp(key):
+            grp[key] = sb.tile([P, 2048], BF16, name="grp_%s" % key, tag="grp", bufs=3, align_bytes=64)
+
+        def quant(codes, scales, key, tag, bufs, src, fmt):
+            codes[key] = sb.tile([P, 512], U32, name="%s%s" % (tag, key), tag=tag, bufs=bufs, align_bytes=64)
+            scales[key] = sb.tile([P, 512], U8, name="%ss%s" % (tag, key), tag=tag + "s", bufs=bufs, align_bytes=64)
+            nc.vector.quantize_mx(out=codes[key][:].bitcast(fmt), scales=scales[key][:], in_=src)
+
+        def sq(u):
+            st[u] = sb.tile([P, 2, 4, 256], F32, name="s%d" % u, tag="s", bufs=4)
+            nc.scalar.activation(out=flat(st[u]), in_=flat(zt[u]), func=AF.Square)
+
+        def ln(u):
+            lt[u] = sb.tile([P, 2, 4, 256], F32, name="l%d" % u, tag="l", bufs=3)
+            nc.scalar.activation(out=flat(lt[u]), in_=flat(st[u]), func=AF.Ln)
+
+        def ee(u):
+            nc.scalar.activation(out=flat(st[u]), in_=flat(st[u]), func=AF.Exp, scale=-0.5)
+
+        def rs(u):
+            nc.scalar.activation(out=flat(lt[u]), in_=flat(lt[u]), func=AF.Exp, scale=-1.0)
+
+        def ge(u):
+            at[u] = sb.tile([P, 2, 4, 256], F32, name="a%d" % u, tag="a", bufs=5)
+            nc.scalar.activation(out=flat(at[u]), in_=flat(zt[u]), func=AF.Gelu)
+
+        def ev_t(u):
+            new_grp("t%d" % u)
+            for h in range(2):
+                empty_bank(nc.scalar.copy, "t%d_%d" % (u, h), grp["t%d" % u], h)
+
+        def ev_1(i):
+            for jj in range(4):
+                o1s = sb.tile([P, 512], F32, name="o1s%d_%d" % (i, jj), tag="o1s", bufs=4)
+                nc.scalar.copy(out=o1s[:].rearrange("q (m j) -> q m j", j=4), in_=o1[(i, jj)][:].rearrange("q (j m) -> q m j", j=4))
+                nc.sync.dma_start(out=out_1[i].rearrange("(m t) k -> m t k", t=4)[:, jj, :], in_=o1s[:])
+
+        def gp(u):
+            eng = nc.gpsimd if GP_ON_POOL else nc.vector
+            eng.tensor_tensor(out=flat(zt[u]), in0=flat(zt[u]), in1=flat(gt[u]), op=ALU.mult)
+
+        def k1(u):
+            nc.vector.tensor_tensor(out=flat(at[u]), in0=flat(at[u]), in1=flat(lt[u]), op=ALU.mult)
+
+        def k2(u):
+            nc.vector.scalar_tensor_tensor(out=flat(at[u]), in0=flat(st[u]), scalar=INV_SQRT_2PI, in1=flat(at[u]), op0=ALU.mult, op1=ALU.add)
+
+        def dz(u):
+            nc.vector.tensor_tensor(out=flat(at[u]), in0=flat(at[u]), in1=flat(zt[u]), op=ALU.mult)
+
+        def castn(u):
+            dzb[u] = sb.tile([P, 4, 512], BF16, name="dzb%d" % u, tag="dzb", bufs=2)
+            nc.vector.tensor_copy(out=dzb[u][:].rearrange("p j (b t) -> p b j t", b=2), in_=at[u][:])
+
+        def casti(u):
+            gk[u] = sb.tile([P, 512, 4], BF16, name="gk%d" % u, tag="gk", bufs=1, align_bytes=64)
+            nc.vector.tensor_copy(out=gk[u][:], in_=dzb[u][:].rearrange("p j t -> p t j"))
+
+        def qk(u):
+            quant(kq, ks, u, "kq", 2, gk[u][:].rearrange("p t j -> p (t j)"), E5)
+
+        def qt(u):
+            quant(tq, ts, u, "tq", 4, grp["t%d" % u][:], E5)
+
+        def res(u, t):
+            nc.vector.tensor_tensor(out=at[u][:, :, t, :], in0=o0[(u, t)][:].rearrange("p (b t) -> p b t", b=2), in1=at[u][:, :, t, :], op=ALU.add)
+
+        def store0(u):
+            nc.sync.dma_start(out=unit_view(out_0, u), in_=at[u][:].rearrange("p b j t -> p b (j t)"))
+
+        def tp_t(u):
+            for h in range(2):
+                fill_bank("t%d_%d" % (u, h), dzb[u], h)
+
+        def mm0(u, t):
+            i = u // 2
+            o0[(u, t)] = psum.tile([P, 512], F32, name="o0_%d_%d" % (u, t), tag="o0", bufs=2)
+            c = slice(128 * t, 128 * (t + 1))
+            nc.tensor.matmul_mx(out=o0[(u, t)][:], lhsT=wq[i][:, c].bitcast(E4), lhsT_scale=ws[i][:, c], rhs=kq[u][:].bitcast(E5), rhs_scale=ks[u][:], start=True, stop=True)
+
+        def mm1(i):
+            for jj in range(4):
+                o1[(i, jj)] = psum.tile([P, 512], F32, name="o1_%d_%d" % (i, jj), tag="o1", bufs=4)
+                c = slice(128 * jj, 128 * (jj + 1))
+                for g in range(2):
+                    u = 2 * i + g
+                    nc.tensor.matmul_mx(out=o1[(i, jj)][:], lhsT=xq[u][:, c].bitcast(E4), lhsT_scale=xs[u][:, c], rhs=tq[u][:].bitcast(E5), rhs_scale=ts[u][:], start=(g == 0), stop=(g == 1))
+
+        ident = const.tile([P, P], F32, name="ident")
+        make_identity(nc, ident[:])
+        warm = const.tile([P, 1], F32, name="warm")
+        nc.vector.memset(warm[:], 1.0)
+        nc.scalar.activation(out=warm[:], in_=warm[:], func=AF.Ln)
+
+        load_z(0)
+        load_raw(0)
+        load_raw(1)
+        load_z(1)
+        load_raw(2)
+
+        for f, us in ((sq, (0, 1)), (ln, (0, 1))):
+            for u in us:
+                f(u)
+        for u in (0, 1):
+            ee(u)
+            rs(u)
+        ge(0)
+        ge(1)
+
+        extra = {0: (load_g, 0), 2: (load_g, 1), 4: (load_z, 2), 6: (load_z, 3), 8: (load_g, 2)}
+        nb = 2 * len(RAW)
+
+        def head_quant(r):
+            kind, n = RAW[r]
+            if kind == "w":
+                quant(wq, ws, n, "wq", 4, grp["r%d" % r][:], E4)
+            else:
+                quant(xq, xs, n, "xq", 8, grp["r%d" % r][:], E4)
+
+        for k in range(nb + 3):
+            if k < nb:
+                fill_bank("r%d" % k, raw[k // 2], k % 2)
+                if k % 2 == 1:
+                    r = k // 2
+                    if r + 3 < len(RAW):
+                        load_raw(r + 3)
+                    if r in extra:
+                        extra[r][0](extra[r][1])
+            if 1 <= k <= nb:
+                if (k - 1) % 2 == 0:
+                    new_grp("r%d" % ((k - 1) // 2))
+                empty_bank(nc.vector.tensor_copy, "r%d" % (k - 1), grp["r%d" % ((k - 1) // 2)], (k - 1) % 2)
+            if k >= 3 and k % 2 == 1:
+                head_quant((k - 3) // 2)
+
+        for u in (2, 3):
+            ge(u)
+        for u in (2, 3):
+            sq(u)
+        ln(2)
+
+        batch = {
+            0: ((ln, 3), (ev_t, 0), (ee, 2), (rs, 2), (ee, 3), (rs, 3), (sq, 4)),
+            1: ((ev_t, 1), (sq, 5), (ln, 4)),
+            2: ((ln, 5), (ee, 4), (rs, 4), (ev_t, 2), (ee, 5), (rs, 5), (ev_1, 0), (ge, 4), (ge, 5), (ge, 6)),
+            3: ((ev_t, 3), (ge, 7), (sq, 6), (sq, 7), (ln, 6)),
+            4: ((ln, 7), (ee, 6), (rs, 6), (ev_t, 4), (ee, 7), (rs, 7), (ev_1, 1)),
+            5: ((ev_t, 5),),
+            6: ((ev_t, 6), (ev_1, 2)),
+            7: ((ev_t, 7),),
+            8: ((ev_1, 3),),
+        }
+
+        gp(0)
+        for n in range(UNITS + 1):
+            cur = n < UNITS
+            old = n >= 1
+            if cur:
+                k1(n)
+            if old:
+                res(n - 1, 0)
+                mm0(n - 1, 2)
+            if cur:
+                k2(n)
+            if old:
+                res(n - 1, 1)
+                mm0(n - 1, 3)
+            if cur:
+                dz(n)
+            if old:
+                res(n - 1, 2)
+            if cur:
+                castn(n)
+                tp_t(n)
+            if old:
+                res(n - 1, 3)
+                store0(n - 1)
+            if cur:
+                casti(n)
+            if old:
+                qt(n - 1)
+                if (n - 1) % 2 == 1:
+                    mm1((n - 1) // 2)
+            if n + 1 < UNITS:
+                gp(n + 1)
+            if cur:
+                qk(n)
+                mm0(n, 0)
+                mm0(n, 1)
+            if n + 4 < UNITS:
+                load_z(n + 4)
+            if n + 3 < UNITS:
+                load_g(n + 3)
+            for f, arg in batch[n]:
+                f(arg)

@@ -19,7 +19,8 @@ UNITS = 8
 FLOPS = 2 * 2 * CB * CD * CD * 1024
 INV_SQRT_2PI = 0.3989422804014327
 
-GP_ON_POOL = False
+HEAD_RAWS = 6
+CASTN_ACT = (5, 6, 7)
 
 
 def tile_spectralchannelmixing_v_kernel(tc, x, wc, z, grad_out, out_0, out_1):
@@ -54,7 +55,7 @@ def tile_spectralchannelmixing_v_kernel(tc, x, wc, z, grad_out, out_0, out_1):
 
         def load_raw(r):
             kind, n = RAW[r]
-            raw[r] = sb.tile([P, 4, 512], BF16, name="raw%d" % r, tag="raw", bufs=3)
+            raw[r] = sb.tile([P, 4, 512], BF16, name="raw%d" % r, tag="raw", bufs=5)
             if kind == "w":
                 nc.sync.dma_start(out=raw[r][:], in_=wc[n].rearrange("(m t) k -> m t k", t=4))
             else:
@@ -65,9 +66,9 @@ def tile_spectralchannelmixing_v_kernel(tc, x, wc, z, grad_out, out_0, out_1):
                         in_=x[2 * g + bb, CD * i : CD * (i + 1)].rearrange("(p j) h w -> p j (h w)", j=4),
                     )
 
-        def fill_bank(key, src, h):
+        def fill_bank(key, src, h, tag):
             words = src[:].rearrange("p j t -> p (j t)").bitcast(F32)
-            banks[key] = psum.tile([P, 512], F32, name="tp_%s" % key, tag="tp", bufs=2)
+            banks[key] = psum.tile([P, 512], F32, name="tp_%s" % key, tag=tag, bufs=2)
             for jj in range(2):
                 for w in range(2):
                     j = 2 * h + jj
@@ -79,7 +80,7 @@ def tile_spectralchannelmixing_v_kernel(tc, x, wc, z, grad_out, out_0, out_1):
             eng_copy(out=out, in_=banks[key][:].rearrange("q (j w m) -> q j m w", j=2, w=2))
 
         def new_grp(key):
-            grp[key] = sb.tile([P, 2048], BF16, name="grp_%s" % key, tag="grp", bufs=3, align_bytes=64)
+            grp[key] = sb.tile([P, 2048], BF16, name="grp_%s" % key, tag="grp", bufs=2, align_bytes=64)
 
         def quant(codes, scales, key, tag, bufs, src, fmt):
             codes[key] = sb.tile([P, 512], U32, name="%s%s" % (tag, key), tag=tag, bufs=bufs, align_bytes=64)
@@ -107,17 +108,23 @@ def tile_spectralchannelmixing_v_kernel(tc, x, wc, z, grad_out, out_0, out_1):
         def ev_t(u):
             new_grp("t%d" % u)
             for h in range(2):
-                empty_bank(nc.scalar.copy, "t%d_%d" % (u, h), grp["t%d" % u], h)
+                empty_bank(nc.vector.tensor_copy, "t%d_%d" % (u, h), grp["t%d" % u], h)
 
-        def ev_1(i):
-            for jj in range(4):
-                o1s = sb.tile([P, 512], F32, name="o1s%d_%d" % (i, jj), tag="o1s", bufs=4)
-                nc.scalar.copy(out=o1s[:].rearrange("q (m j) -> q m j", j=4), in_=o1[(i, jj)][:].rearrange("q (j m) -> q m j", j=4))
-                nc.sync.dma_start(out=out_1[i].rearrange("(m t) k -> m t k", t=4)[:, jj, :], in_=o1s[:])
+        def ev_1(eng_copy, i, jj):
+            o1s = sb.tile([P, 512], F32, name="o1s%d_%d" % (i, jj), tag="o1s", bufs=4)
+            eng_copy(out=o1s[:].rearrange("q (m j) -> q m j", j=4), in_=o1[(i, jj)][:].rearrange("q (j m) -> q m j", j=4))
+            nc.sync.dma_start(out=out_1[i].rearrange("(m t) k -> m t k", t=4)[:, jj, :], in_=o1s[:])
+
+        def ev_1_act(half):
+            for jj in (2 * (half % 2), 2 * (half % 2) + 1):
+                ev_1(nc.scalar.copy, half // 2, jj)
+
+        def sq_dve(u):
+            st[u] = sb.tile([P, 2, 4, 256], F32, name="s%d" % u, tag="s", bufs=4)
+            nc.vector.tensor_tensor(out=flat(st[u]), in0=flat(zt[u]), in1=flat(zt[u]), op=ALU.mult)
 
         def gp(u):
-            eng = nc.gpsimd if GP_ON_POOL else nc.vector
-            eng.tensor_tensor(out=flat(zt[u]), in0=flat(zt[u]), in1=flat(gt[u]), op=ALU.mult)
+            nc.vector.tensor_tensor(out=flat(zt[u]), in0=flat(zt[u]), in1=flat(gt[u]), op=ALU.mult)
 
         def k1(u):
             nc.vector.tensor_tensor(out=flat(at[u]), in0=flat(at[u]), in1=flat(lt[u]), op=ALU.mult)
@@ -126,15 +133,16 @@ def tile_spectralchannelmixing_v_kernel(tc, x, wc, z, grad_out, out_0, out_1):
             nc.vector.scalar_tensor_tensor(out=flat(at[u]), in0=flat(st[u]), scalar=INV_SQRT_2PI, in1=flat(at[u]), op0=ALU.mult, op1=ALU.add)
 
         def dz(u):
-            nc.vector.tensor_tensor(out=flat(at[u]), in0=flat(at[u]), in1=flat(zt[u]), op=ALU.mult)
+            nc.gpsimd.tensor_tensor(out=flat(at[u]), in0=flat(at[u]), in1=flat(zt[u]), op=ALU.mult)
 
         def castn(u):
             dzb[u] = sb.tile([P, 4, 512], BF16, name="dzb%d" % u, tag="dzb", bufs=2)
-            nc.vector.tensor_copy(out=dzb[u][:].rearrange("p j (b t) -> p b j t", b=2), in_=at[u][:])
+            eng_copy = nc.scalar.copy if u in CASTN_ACT else nc.vector.tensor_copy
+            eng_copy(out=dzb[u][:].rearrange("p j (b t) -> p b j t", b=2), in_=at[u][:])
 
         def casti(u):
             gk[u] = sb.tile([P, 512, 4], BF16, name="gk%d" % u, tag="gk", bufs=1, align_bytes=64)
-            nc.vector.tensor_copy(out=gk[u][:], in_=dzb[u][:].rearrange("p j t -> p t j"))
+            nc.vector.tensor_copy(out=gk[u][:].rearrange("p (b t) j -> p b t j", b=2), in_=at[u][:].rearrange("p b j t -> p b t j"))
 
         def qk(u):
             quant(kq, ks, u, "kq", 2, gk[u][:].rearrange("p t j -> p (t j)"), E5)
@@ -150,7 +158,7 @@ def tile_spectralchannelmixing_v_kernel(tc, x, wc, z, grad_out, out_0, out_1):
 
         def tp_t(u):
             for h in range(2):
-                fill_bank("t%d_%d" % (u, h), dzb[u], h)
+                fill_bank("t%d_%d" % (u, h), dzb[u], h, "tp")
 
         def mm0(u, t):
             i = u // 2
@@ -158,9 +166,10 @@ def tile_spectralchannelmixing_v_kernel(tc, x, wc, z, grad_out, out_0, out_1):
             c = slice(128 * t, 128 * (t + 1))
             nc.tensor.matmul_mx(out=o0[(u, t)][:], lhsT=wq[i][:, c].bitcast(E4), lhsT_scale=ws[i][:, c], rhs=kq[u][:].bitcast(E5), rhs_scale=ks[u][:], start=True, stop=True)
 
-        def mm1(i):
-            for jj in range(4):
-                o1[(i, jj)] = psum.tile([P, 512], F32, name="o1_%d_%d" % (i, jj), tag="o1", bufs=4)
+        def mm1(half, tag):
+            i = half // 2
+            for jj in (2 * (half % 2), 2 * (half % 2) + 1):
+                o1[(i, jj)] = psum.tile([P, 512], F32, name="o1_%d_%d" % (i, jj), tag=tag, bufs=2)
                 c = slice(128 * jj, 128 * (jj + 1))
                 for g in range(2):
                     u = 2 * i + g
@@ -170,99 +179,118 @@ def tile_spectralchannelmixing_v_kernel(tc, x, wc, z, grad_out, out_0, out_1):
         make_identity(nc, ident[:])
         warm = const.tile([P, 1], F32, name="warm")
         nc.vector.memset(warm[:], 1.0)
-        nc.scalar.activation(out=warm[:], in_=warm[:], func=AF.Ln)
+        nc.scalar.activation(out=warm[:], in_=warm[:], func=AF.Gelu)
 
-        load_z(0)
-        load_raw(0)
-        load_raw(1)
-        load_z(1)
-        load_raw(2)
+        def raw_fill(r, h):
+            fill_bank("r%d_%d" % (r, h), raw[r], h, "tr")
 
-        for f, us in ((sq, (0, 1)), (ln, (0, 1))):
-            for u in us:
-                f(u)
-        for u in (0, 1):
-            ee(u)
-            rs(u)
-        ge(0)
-        ge(1)
+        def raw_empty(r, h):
+            if h == 0:
+                new_grp("r%d" % r)
+            empty_bank(nc.vector.tensor_copy, "r%d_%d" % (r, h), grp["r%d" % r], h)
 
-        extra = {0: (load_g, 0), 2: (load_g, 1), 4: (load_z, 2), 6: (load_z, 3), 8: (load_g, 2)}
-        nb = 2 * len(RAW)
-
-        def head_quant(r):
+        def raw_quant(r):
             kind, n = RAW[r]
             if kind == "w":
                 quant(wq, ws, n, "wq", 4, grp["r%d" % r][:], E4)
             else:
                 quant(xq, xs, n, "xq", 8, grp["r%d" % r][:], E4)
 
+        load_z(0)
+        load_z(1)
+        for r in range(3):
+            load_raw(r)
+        load_g(0)
+        for r in range(3, 5):
+            load_raw(r)
+        load_g(1)
+
+        def act_half(n):
+            v = n // 2 + 1
+            if 2 * v >= UNITS:
+                return
+            if n % 2 == 0:
+                ge(2 * v)
+                ge(2 * v + 1)
+                sq(2 * v)
+                sq(2 * v + 1)
+                ln(2 * v)
+            else:
+                ln(2 * v + 1)
+                for u in (2 * v, 2 * v + 1):
+                    ee(u)
+                    rs(u)
+
+        ge(0)
+        ge(1)
+        sq_dve(0)
+        sq_dve(1)
+        ln(0)
+        ln(1)
+        for u in (0, 1):
+            ee(u)
+            rs(u)
+
+        late = {1: (load_z, 2), 3: (load_z, 3), 5: (load_g, 2)}
+        nb = 2 * HEAD_RAWS
         for k in range(nb + 3):
             if k < nb:
-                fill_bank("r%d" % k, raw[k // 2], k % 2)
-                if k % 2 == 1:
-                    r = k // 2
-                    if r + 3 < len(RAW):
-                        load_raw(r + 3)
-                    if r in extra:
-                        extra[r][0](extra[r][1])
+                raw_fill(k // 2, k % 2)
+                if k % 2 == 1 and k // 2 + 5 < len(RAW):
+                    load_raw(k // 2 + 5)
+                if k in late:
+                    late[k][0](late[k][1])
             if 1 <= k <= nb:
-                if (k - 1) % 2 == 0:
-                    new_grp("r%d" % ((k - 1) // 2))
-                empty_bank(nc.vector.tensor_copy, "r%d" % (k - 1), grp["r%d" % ((k - 1) // 2)], (k - 1) % 2)
+                raw_empty((k - 1) // 2, (k - 1) % 2)
             if k >= 3 and k % 2 == 1:
-                head_quant((k - 3) // 2)
+                raw_quant((k - 3) // 2)
 
-        for u in (2, 3):
-            ge(u)
-        for u in (2, 3):
-            sq(u)
-        ln(2)
-
-        batch = {
-            0: ((ln, 3), (ev_t, 0), (ee, 2), (rs, 2), (ee, 3), (rs, 3), (sq, 4)),
-            1: ((ev_t, 1), (sq, 5), (ln, 4)),
-            2: ((ln, 5), (ee, 4), (rs, 4), (ev_t, 2), (ee, 5), (rs, 5), (ev_1, 0), (ge, 4), (ge, 5), (ge, 6)),
-            3: ((ev_t, 3), (ge, 7), (sq, 6), (sq, 7), (ln, 6)),
-            4: ((ln, 7), (ee, 6), (rs, 6), (ev_t, 4), (ee, 7), (rs, 7), (ev_1, 1)),
-            5: ((ev_t, 5),),
-            6: ((ev_t, 6), (ev_1, 2)),
-            7: ((ev_t, 7),),
-            8: ((ev_1, 3),),
-        }
-
-        gp(0)
         for n in range(UNITS + 1):
             cur = n < UNITS
             old = n >= 1
+            r = HEAD_RAWS + n
+            has_raw = r < len(RAW)
+            if old and (n - 1) in CASTN_ACT:
+                castn(n - 1)
+                tp_t(n - 1)
+            if 3 <= n:
+                ev_1_act(n - 3)
+            act_half(n)
+            if has_raw:
+                raw_fill(r, 0)
+                raw_fill(r, 1)
+                if r + 5 < len(RAW):
+                    load_raw(r + 5)
             if cur:
                 k1(n)
-            if old:
-                res(n - 1, 0)
-                mm0(n - 1, 2)
-            if cur:
+                gp(n)
                 k2(n)
-            if old:
-                res(n - 1, 1)
-                mm0(n - 1, 3)
-            if cur:
                 dz(n)
             if old:
+                res(n - 1, 0)
+                res(n - 1, 1)
+                mm0(n - 1, 2)
+                mm0(n - 1, 3)
+                ev_t(n - 1)
                 res(n - 1, 2)
-            if cur:
+                res(n - 1, 3)
+                store0(n - 1)
+            if has_raw:
+                raw_empty(r, 0)
+                raw_empty(r, 1)
+            if cur and n not in CASTN_ACT:
                 castn(n)
                 tp_t(n)
             if old:
-                res(n - 1, 3)
-                store0(n - 1)
+                qt(n - 1)
+            if n >= 2:
+                mm1(n - 2, "o1")
+            if n == UNITS:
+                mm1(n - 1, "tr")
             if cur:
                 casti(n)
-            if old:
-                qt(n - 1)
-                if (n - 1) % 2 == 1:
-                    mm1((n - 1) // 2)
-            if n + 1 < UNITS:
-                gp(n + 1)
+            if has_raw:
+                raw_quant(r)
             if cur:
                 qk(n)
                 mm0(n, 0)
@@ -271,5 +299,7 @@ def tile_spectralchannelmixing_v_kernel(tc, x, wc, z, grad_out, out_0, out_1):
                 load_z(n + 4)
             if n + 3 < UNITS:
                 load_g(n + 3)
-            for f, arg in batch[n]:
-                f(arg)
+        ev_1(nc.scalar.copy, 3, 0)
+        ev_1(nc.vector.tensor_copy, 3, 1)
+        ev_1(nc.scalar.copy, 3, 2)
+        ev_1(nc.vector.tensor_copy, 3, 3)

@@ -19,8 +19,9 @@ UNITS = 8
 FLOPS = 2 * 2 * CB * CD * CD * 1024
 INV_SQRT_2PI = 0.3989422804014327
 
-HEAD_RAWS = 6
-CASTN_ACT = (5, 6, 7)
+HEAD_RAWS = 5
+LATE = 6
+POOL_GP = ()
 
 
 def tile_spectralchannelmixing_v_kernel(tc, x, wc, z, grad_out, out_0, out_1):
@@ -108,7 +109,7 @@ def tile_spectralchannelmixing_v_kernel(tc, x, wc, z, grad_out, out_0, out_1):
         def ev_t(u):
             new_grp("t%d" % u)
             for h in range(2):
-                empty_bank(nc.vector.tensor_copy, "t%d_%d" % (u, h), grp["t%d" % u], h)
+                empty_bank(nc.scalar.copy if u + 1 >= LATE else nc.vector.tensor_copy, "t%d_%d" % (u, h), grp["t%d" % u], h)
 
         def ev_1(eng_copy, i, jj):
             o1s = sb.tile([P, 512], F32, name="o1s%d_%d" % (i, jj), tag="o1s", bufs=4)
@@ -124,7 +125,8 @@ def tile_spectralchannelmixing_v_kernel(tc, x, wc, z, grad_out, out_0, out_1):
             nc.vector.tensor_tensor(out=flat(st[u]), in0=flat(zt[u]), in1=flat(zt[u]), op=ALU.mult)
 
         def gp(u):
-            nc.vector.tensor_tensor(out=flat(zt[u]), in0=flat(zt[u]), in1=flat(gt[u]), op=ALU.mult)
+            eng = nc.gpsimd if u in POOL_GP else nc.vector
+            eng.tensor_tensor(out=flat(zt[u]), in0=flat(zt[u]), in1=flat(gt[u]), op=ALU.mult)
 
         def k1(u):
             nc.vector.tensor_tensor(out=flat(at[u]), in0=flat(at[u]), in1=flat(lt[u]), op=ALU.mult)
@@ -133,16 +135,18 @@ def tile_spectralchannelmixing_v_kernel(tc, x, wc, z, grad_out, out_0, out_1):
             nc.vector.scalar_tensor_tensor(out=flat(at[u]), in0=flat(st[u]), scalar=INV_SQRT_2PI, in1=flat(at[u]), op0=ALU.mult, op1=ALU.add)
 
         def dz(u):
-            nc.gpsimd.tensor_tensor(out=flat(at[u]), in0=flat(at[u]), in1=flat(zt[u]), op=ALU.mult)
+            eng = nc.vector if u >= LATE else nc.gpsimd
+            eng.tensor_tensor(out=flat(at[u]), in0=flat(at[u]), in1=flat(zt[u]), op=ALU.mult)
 
         def castn(u):
             dzb[u] = sb.tile([P, 4, 512], BF16, name="dzb%d" % u, tag="dzb", bufs=2)
-            eng_copy = nc.scalar.copy if u in CASTN_ACT else nc.vector.tensor_copy
+            eng_copy = nc.scalar.copy if u in (LATE - 1, LATE) else nc.vector.tensor_copy
             eng_copy(out=dzb[u][:].rearrange("p j (b t) -> p b j t", b=2), in_=at[u][:])
 
         def casti(u):
             gk[u] = sb.tile([P, 512, 4], BF16, name="gk%d" % u, tag="gk", bufs=1, align_bytes=64)
-            nc.vector.tensor_copy(out=gk[u][:].rearrange("p (b t) j -> p b t j", b=2), in_=at[u][:].rearrange("p b j t -> p b t j"))
+            eng_copy = nc.scalar.copy if u >= LATE else nc.vector.tensor_copy
+            eng_copy(out=gk[u][:].rearrange("p (b t) j -> p b t j", b=2), in_=at[u][:].rearrange("p b j t -> p b t j"))
 
         def qk(u):
             quant(kq, ks, u, "kq", 2, gk[u][:].rearrange("p t j -> p (t j)"), E5)
@@ -203,13 +207,14 @@ def tile_spectralchannelmixing_v_kernel(tc, x, wc, z, grad_out, out_0, out_1):
         load_g(0)
         for r in range(3, 5):
             load_raw(r)
-        load_g(1)
 
         def act_half(n):
             v = n // 2 + 1
             if 2 * v >= UNITS:
                 return
             if n % 2 == 0:
+                if n == 0:
+                    ge(1)
                 ge(2 * v)
                 ge(2 * v + 1)
                 sq(2 * v)
@@ -222,7 +227,6 @@ def tile_spectralchannelmixing_v_kernel(tc, x, wc, z, grad_out, out_0, out_1):
                     rs(u)
 
         ge(0)
-        ge(1)
         sq_dve(0)
         sq_dve(1)
         ln(0)
@@ -230,55 +234,77 @@ def tile_spectralchannelmixing_v_kernel(tc, x, wc, z, grad_out, out_0, out_1):
         for u in (0, 1):
             ee(u)
             rs(u)
+        for u in POOL_GP:
+            gp(u)
 
-        late = {1: (load_z, 2), 3: (load_z, 3), 5: (load_g, 2)}
+        late_loads = {3: (load_z, 2), 5: (load_z, 3), 7: (load_g, 1)}
         nb = 2 * HEAD_RAWS
         for k in range(nb + 3):
             if k < nb:
                 raw_fill(k // 2, k % 2)
                 if k % 2 == 1 and k // 2 + 5 < len(RAW):
                     load_raw(k // 2 + 5)
-                if k in late:
-                    late[k][0](late[k][1])
+                if k in late_loads:
+                    late_loads[k][0](late_loads[k][1])
             if 1 <= k <= nb:
                 raw_empty((k - 1) // 2, (k - 1) % 2)
             if k >= 3 and k % 2 == 1:
                 raw_quant((k - 3) // 2)
 
+        gp(0)
+        step_raws = {0: (5, 6, 7), 1: (8,), 2: (9,), 3: (10,), 4: (11,)}
+
         for n in range(UNITS + 1):
             cur = n < UNITS
             old = n >= 1
-            r = HEAD_RAWS + n
-            has_raw = r < len(RAW)
-            if old and (n - 1) in CASTN_ACT:
+            late = n >= LATE
+            raws = step_raws.get(n, ())
+            if n == LATE:
                 castn(n - 1)
                 tp_t(n - 1)
-            if 3 <= n:
+            if 3 <= n and n != LATE - 1:
                 ev_1_act(n - 3)
+            if late:
+                ev_t(n - 1)
             act_half(n)
-            if has_raw:
-                raw_fill(r, 0)
-                raw_fill(r, 1)
-                if r + 5 < len(RAW):
-                    load_raw(r + 5)
+            if raws:
+                raw_fill(raws[0], 0)
+                raw_fill(raws[0], 1)
             if cur:
                 k1(n)
-                gp(n)
+                if n > 0:
+                    gp(n)
                 k2(n)
                 dz(n)
+            if cur and late:
+                if n == UNITS - 1:
+                    castn(n)
+                casti(n)
+                if n < UNITS - 1:
+                    castn(n)
             if old:
                 res(n - 1, 0)
                 res(n - 1, 1)
                 mm0(n - 1, 2)
                 mm0(n - 1, 3)
-                ev_t(n - 1)
+                if not late:
+                    ev_t(n - 1)
                 res(n - 1, 2)
                 res(n - 1, 3)
                 store0(n - 1)
-            if has_raw:
-                raw_empty(r, 0)
-                raw_empty(r, 1)
-            if cur and n not in CASTN_ACT:
+            if n == LATE - 1:
+                for jj in (0, 1):
+                    ev_1(nc.vector.tensor_copy, (n - 3) // 2, 2 * ((n - 3) % 2) + jj)
+            for q in range(len(raws)):
+                for h in range(2):
+                    raw_empty(raws[q], h)
+                    if q + 1 < len(raws):
+                        raw_fill(raws[q + 1], h)
+                if raws[q] + 5 < len(RAW):
+                    load_raw(raws[q] + 5)
+                if q + 1 < len(raws):
+                    raw_quant(raws[q])
+            if cur and n < LATE - 1:
                 castn(n)
                 tp_t(n)
             if old:
@@ -287,18 +313,20 @@ def tile_spectralchannelmixing_v_kernel(tc, x, wc, z, grad_out, out_0, out_1):
                 mm1(n - 2, "o1")
             if n == UNITS:
                 mm1(n - 1, "tr")
-            if cur:
+            if cur and not late:
                 casti(n)
-            if has_raw:
-                raw_quant(r)
+            if raws:
+                raw_quant(raws[-1])
             if cur:
                 qk(n)
                 mm0(n, 0)
                 mm0(n, 1)
+            if cur and late:
+                tp_t(n)
             if n + 4 < UNITS:
                 load_z(n + 4)
-            if n + 3 < UNITS:
-                load_g(n + 3)
+            if n + 2 < UNITS:
+                load_g(n + 2)
         ev_1(nc.scalar.copy, 3, 0)
         ev_1(nc.vector.tensor_copy, 3, 1)
         ev_1(nc.scalar.copy, 3, 2)

@@ -140,7 +140,7 @@ def tile_spectralchannelmixing_v_kernel(tc, x, wc, z, grad_out, out_0, out_1):
 
         def castn(u):
             dzb[u] = sb.tile([P, 4, 512], BF16, name="dzb%d" % u, tag="dzb", bufs=2)
-            eng_copy = nc.scalar.copy if u in (LATE - 1, LATE) else nc.vector.tensor_copy
+            eng_copy = nc.scalar.copy if u == LATE else nc.vector.tensor_copy
             eng_copy(out=dzb[u][:].rearrange("p j (b t) -> p b j t", b=2), in_=at[u][:])
 
         def casti(u):
@@ -156,6 +156,9 @@ def tile_spectralchannelmixing_v_kernel(tc, x, wc, z, grad_out, out_0, out_1):
 
         def res(u, t):
             nc.vector.tensor_tensor(out=at[u][:, :, t, :], in0=o0[(u, t)][:].rearrange("p (b t) -> p b t", b=2), in1=at[u][:, :, t, :], op=ALU.add)
+
+        def store0_slot(u, t):
+            nc.sync.dma_start(out=unit_view(out_0, u)[:, :, 256 * t : 256 * (t + 1)], in_=at[u][:, :, t, :])
 
         def store0(u):
             nc.sync.dma_start(out=unit_view(out_0, u), in_=at[u][:].rearrange("p b j t -> p b (j t)"))
@@ -254,41 +257,26 @@ def tile_spectralchannelmixing_v_kernel(tc, x, wc, z, grad_out, out_0, out_1):
         gp(0)
         step_raws = {0: (5, 6, 7), 1: (8,), 2: (9,), 3: (10,), 4: (11,)}
 
-        for n in range(UNITS + 1):
-            cur = n < UNITS
+        for n in range(LATE):
             old = n >= 1
-            late = n >= LATE
             raws = step_raws.get(n, ())
-            if n == LATE:
-                castn(n - 1)
-                tp_t(n - 1)
-            if 3 <= n and n != LATE - 1:
+            if 3 <= n < LATE - 1:
                 ev_1_act(n - 3)
-            if late:
-                ev_t(n - 1)
             act_half(n)
             if raws:
                 raw_fill(raws[0], 0)
                 raw_fill(raws[0], 1)
-            if cur:
-                k1(n)
-                if n > 0:
-                    gp(n)
-                k2(n)
-                dz(n)
-            if cur and late:
-                if n == UNITS - 1:
-                    castn(n)
-                casti(n)
-                if n < UNITS - 1:
-                    castn(n)
+            k1(n)
+            if n > 0:
+                gp(n)
+            k2(n)
+            dz(n)
             if old:
                 res(n - 1, 0)
                 res(n - 1, 1)
                 mm0(n - 1, 2)
                 mm0(n - 1, 3)
-                if not late:
-                    ev_t(n - 1)
+                ev_t(n - 1)
                 res(n - 1, 2)
                 res(n - 1, 3)
                 store0(n - 1)
@@ -304,30 +292,65 @@ def tile_spectralchannelmixing_v_kernel(tc, x, wc, z, grad_out, out_0, out_1):
                     load_raw(raws[q] + 5)
                 if q + 1 < len(raws):
                     raw_quant(raws[q])
-            if cur and n < LATE - 1:
-                castn(n)
-                tp_t(n)
             if old:
                 qt(n - 1)
             if n >= 2:
                 mm1(n - 2, "o1")
-            if n == UNITS:
-                mm1(n - 1, "tr")
-            if cur and not late:
-                casti(n)
+            castn(n)
+            tp_t(n)
+            casti(n)
             if raws:
                 raw_quant(raws[-1])
-            if cur:
-                qk(n)
-                mm0(n, 0)
-                mm0(n, 1)
-            if cur and late:
-                tp_t(n)
+            qk(n)
+            mm0(n, 0)
+            mm0(n, 1)
             if n + 4 < UNITS:
                 load_z(n + 4)
             if n + 2 < UNITS:
                 load_g(n + 2)
-        ev_1(nc.scalar.copy, 3, 0)
-        ev_1(nc.vector.tensor_copy, 3, 1)
-        ev_1(nc.scalar.copy, 3, 2)
-        ev_1(nc.vector.tensor_copy, 3, 3)
+
+        for n in range(LATE, UNITS):
+            last = n == UNITS - 1
+            ev_1_act(n - 3)
+            ev_t(n - 1)
+            k1(n)
+            res(n - 1, 0)
+            gp(n)
+            res(n - 1, 1)
+            mm0(n - 1, 2)
+            mm0(n - 1, 3)
+            k2(n)
+            res(n - 1, 2)
+            dz(n)
+            res(n - 1, 3)
+            store0(n - 1)
+            if last:
+                castn(n)
+                tp_t(n)
+            casti(n)
+            if last:
+                ev_t(n)
+            else:
+                castn(n)
+            qt(n - 1)
+            mm1(n - 2, "o1")
+            qk(n)
+            mm0(n, 0)
+            mm0(n, 1)
+            if not last:
+                tp_t(n)
+        n = UNITS
+        ev_1_act(n - 3)
+        qt(n - 1)
+        mm1(n - 2, "o1")
+        for t in range(2):
+            res(n - 1, t)
+            store0_slot(n - 1, t)
+        mm0(n - 1, 2)
+        mm0(n - 1, 3)
+        mm1(n - 1, "tr")
+        ev_1_act(n - 2)
+        for t in range(2, 4):
+            res(n - 1, t)
+            store0_slot(n - 1, t)
+        ev_1_act(n - 1)

@@ -46,7 +46,11 @@ def tile_spectralchannelmixing_v_kernel(tc, x, wc, z, grad_out, out_0, out_1):
 
         def load_z(u):
             zt[u] = sb.tile([P, 2, 4, 256], F32, name="z%d" % u, tag="z", bufs=4)
-            nc.sync.dma_start(out=zt[u][:].rearrange("p b j t -> p b (j t)"), in_=unit_view(z, u))
+            if u == 0:
+                for b in range(2):
+                    nc.sync.dma_start(out=zt[u][:, b, :, :].rearrange("p j t -> p (j t)"), in_=unit_view(z, u)[:, b, :])
+            else:
+                nc.sync.dma_start(out=zt[u][:].rearrange("p b j t -> p b (j t)"), in_=unit_view(z, u))
 
         def load_g(u):
             gt[u] = sb.tile([P, 2, 4, 256], BF16, name="g%d" % u, tag="g", bufs=3)
@@ -104,7 +108,11 @@ def tile_spectralchannelmixing_v_kernel(tc, x, wc, z, grad_out, out_0, out_1):
 
         def ge(u):
             at[u] = sb.tile([P, 2, 4, 256], F32, name="a%d" % u, tag="a", bufs=5)
-            nc.scalar.activation(out=flat(at[u]), in_=flat(zt[u]), func=AF.Gelu)
+            if u == 0:
+                for b in range(2):
+                    nc.scalar.activation(out=flat(at[u])[:, 1024 * b : 1024 * (b + 1)], in_=flat(zt[u])[:, 1024 * b : 1024 * (b + 1)], func=AF.Gelu)
+            else:
+                nc.scalar.activation(out=flat(at[u]), in_=flat(zt[u]), func=AF.Gelu)
 
         def ev_t(u):
             new_grp("t%d" % u)
@@ -122,7 +130,8 @@ def tile_spectralchannelmixing_v_kernel(tc, x, wc, z, grad_out, out_0, out_1):
 
         def sq_dve(u):
             st[u] = sb.tile([P, 2, 4, 256], F32, name="s%d" % u, tag="s", bufs=4)
-            nc.vector.tensor_tensor(out=flat(st[u]), in0=flat(zt[u]), in1=flat(zt[u]), op=ALU.mult)
+            for c in ((0, 1024), (1024, 2048)) if u == 0 else ((0, 2048),):
+                nc.vector.tensor_tensor(out=flat(st[u])[:, c[0] : c[1]], in0=flat(zt[u])[:, c[0] : c[1]], in1=flat(zt[u])[:, c[0] : c[1]], op=ALU.mult)
 
         def gp(u):
             eng = nc.gpsimd if u in POOL_GP else nc.vector
@@ -140,13 +149,17 @@ def tile_spectralchannelmixing_v_kernel(tc, x, wc, z, grad_out, out_0, out_1):
 
         def castn(u):
             dzb[u] = sb.tile([P, 4, 512], BF16, name="dzb%d" % u, tag="dzb", bufs=2)
-            eng_copy = nc.scalar.copy if u == LATE else nc.vector.tensor_copy
+            eng_copy = nc.scalar.copy if u in (LATE - 1, LATE) else nc.vector.tensor_copy
             eng_copy(out=dzb[u][:].rearrange("p j (b t) -> p b j t", b=2), in_=at[u][:])
 
         def casti(u):
             gk[u] = sb.tile([P, 512, 4], BF16, name="gk%d" % u, tag="gk", bufs=1, align_bytes=64)
             eng_copy = nc.scalar.copy if u >= LATE else nc.vector.tensor_copy
-            eng_copy(out=gk[u][:].rearrange("p (b t) j -> p b t j", b=2), in_=at[u][:].rearrange("p b j t -> p b t j"))
+            for b in range(2):
+                eng_copy(
+                    out=gk[u][:, 256 * b : 256 * (b + 1), :].rearrange("p (c i) j -> p c j i", i=4),
+                    in_=at[u][:, b, :, :].rearrange("p j (c i) -> p c j i", i=4),
+                )
 
         def qk(u):
             quant(kq, ks, u, "kq", 2, gk[u][:].rearrange("p t j -> p (t j)"), E5)
@@ -156,9 +169,6 @@ def tile_spectralchannelmixing_v_kernel(tc, x, wc, z, grad_out, out_0, out_1):
 
         def res(u, t):
             nc.vector.tensor_tensor(out=at[u][:, :, t, :], in0=o0[(u, t)][:].rearrange("p (b t) -> p b t", b=2), in1=at[u][:, :, t, :], op=ALU.add)
-
-        def store0_slot(u, t):
-            nc.sync.dma_start(out=unit_view(out_0, u)[:, :, 256 * t : 256 * (t + 1)], in_=at[u][:, :, t, :])
 
         def store0(u):
             nc.sync.dma_start(out=unit_view(out_0, u), in_=at[u][:].rearrange("p b j t -> p b (j t)"))
@@ -257,26 +267,41 @@ def tile_spectralchannelmixing_v_kernel(tc, x, wc, z, grad_out, out_0, out_1):
         gp(0)
         step_raws = {0: (5, 6, 7), 1: (8,), 2: (9,), 3: (10,), 4: (11,)}
 
-        for n in range(LATE):
+        for n in range(UNITS + 1):
+            cur = n < UNITS
             old = n >= 1
+            late = n >= LATE
             raws = step_raws.get(n, ())
-            if 3 <= n < LATE - 1:
+            if n == LATE:
+                castn(n - 1)
+                tp_t(n - 1)
+            if 3 <= n and n != LATE - 1:
                 ev_1_act(n - 3)
+            if late:
+                ev_t(n - 1)
             act_half(n)
             if raws:
                 raw_fill(raws[0], 0)
                 raw_fill(raws[0], 1)
-            k1(n)
-            if n > 0:
-                gp(n)
-            k2(n)
-            dz(n)
+            if cur:
+                k1(n)
+                if n > 0:
+                    gp(n)
+                k2(n)
+                dz(n)
+            if cur and late:
+                if n == UNITS - 1:
+                    castn(n)
+                casti(n)
+                if n < UNITS - 1:
+                    castn(n)
             if old:
                 res(n - 1, 0)
                 res(n - 1, 1)
                 mm0(n - 1, 2)
                 mm0(n - 1, 3)
-                ev_t(n - 1)
+                if not late:
+                    ev_t(n - 1)
                 res(n - 1, 2)
                 res(n - 1, 3)
                 store0(n - 1)
@@ -292,65 +317,30 @@ def tile_spectralchannelmixing_v_kernel(tc, x, wc, z, grad_out, out_0, out_1):
                     load_raw(raws[q] + 5)
                 if q + 1 < len(raws):
                     raw_quant(raws[q])
+            if cur and n < LATE - 1:
+                castn(n)
+                tp_t(n)
             if old:
                 qt(n - 1)
             if n >= 2:
                 mm1(n - 2, "o1")
-            castn(n)
-            tp_t(n)
-            casti(n)
+            if n == UNITS:
+                mm1(n - 1, "tr")
+            if cur and not late:
+                casti(n)
             if raws:
                 raw_quant(raws[-1])
-            qk(n)
-            mm0(n, 0)
-            mm0(n, 1)
+            if cur:
+                qk(n)
+                mm0(n, 0)
+                mm0(n, 1)
+            if cur and late:
+                tp_t(n)
             if n + 4 < UNITS:
                 load_z(n + 4)
             if n + 2 < UNITS:
                 load_g(n + 2)
-
-        for n in range(LATE, UNITS):
-            last = n == UNITS - 1
-            ev_1_act(n - 3)
-            ev_t(n - 1)
-            k1(n)
-            res(n - 1, 0)
-            gp(n)
-            res(n - 1, 1)
-            mm0(n - 1, 2)
-            mm0(n - 1, 3)
-            k2(n)
-            res(n - 1, 2)
-            dz(n)
-            res(n - 1, 3)
-            store0(n - 1)
-            if last:
-                castn(n)
-                tp_t(n)
-            casti(n)
-            if last:
-                ev_t(n)
-            else:
-                castn(n)
-            qt(n - 1)
-            mm1(n - 2, "o1")
-            qk(n)
-            mm0(n, 0)
-            mm0(n, 1)
-            if not last:
-                tp_t(n)
-        n = UNITS
-        ev_1_act(n - 3)
-        qt(n - 1)
-        mm1(n - 2, "o1")
-        for t in range(2):
-            res(n - 1, t)
-            store0_slot(n - 1, t)
-        mm0(n - 1, 2)
-        mm0(n - 1, 3)
-        mm1(n - 1, "tr")
-        ev_1_act(n - 2)
-        for t in range(2, 4):
-            res(n - 1, t)
-            store0_slot(n - 1, t)
-        ev_1_act(n - 1)
+        ev_1(nc.scalar.copy, 3, 0)
+        ev_1(nc.vector.tensor_copy, 3, 1)
+        ev_1(nc.scalar.copy, 3, 2)
+        ev_1(nc.vector.tensor_copy, 3, 3)

from contextlib import ExitStack

import concourse.mybir as mybir
from concourse.masks import make_identity

F32 = mybir.dt.float32
BF16 = mybir.dt.bfloat16
U32 = mybir.dt.uint32
U8 = mybir.dt.uint8
E4 = mybir.dt.float8_e4m3fn_x4
E5 = mybir.dt.float8_e5m2_x4
AF = mybir.ActivationFunctionType
ALU = mybir.AluOpType

P = 128
CB = 4
CD = 512
UNITS = 8
FLOPS = 2 * 2 * CB * CD * CD * 1024
INV_SQRT_2PI = 0.3989422804014327

HEAD_RAWS = 5
LATE = 6
POOL_GP = ()


def tile_spectralchannelmixing_v_kernel(tc, x, wc, z, grad_out, out_0, out_1):
    nc = tc.nc
    with ExitStack() as ctx:
        ctx.enter_context(tc.manual_schedule())
        const = ctx.enter_context(tc.tile_pool(name="const", bufs=1))
        sb = ctx.enter_context(tc.tile_pool(name="sb", bufs=2))
        psum = ctx.enter_context(tc.psum_pool(name="psum", bufs=2))

        zt, gt, at, st, lt = {}, {}, {}, {}, {}
        raw, grp, dzb, gk = {}, {}, {}, {}
        xq, xs, wq, ws, kq, ks, tq, ts = {}, {}, {}, {}, {}, {}, {}, {}
        banks, o0, o1 = {}, {}, {}

        def unit_view(t, u):
            i, g = divmod(u, 2)
            return t[2 * g : 2 * g + 2, CD * i : CD * (i + 1)].rearrange("b (p j) h w -> p b (j h w)", j=4)

        def flat(t):
            return t[:].rearrange("p b j t -> p (b j t)")

        def load_z(u):
            zt[u] = sb.tile([P, 2, 4, 256], F32, name="z%d" % u, tag="z", bufs=4)
            if u == 0:
                for b in range(2):
                    nc.sync.dma_start(out=zt[u][:, b, :, :].rearrange("p j t -> p (j t)"), in_=unit_view(z, u)[:, b, :])
            else:
                nc.sync.dma_start(out=zt[u][:].rearrange("p b j t -> p b (j t)"), in_=unit_view(z, u))

        def load_g(u):
            gt[u] = sb.tile([P, 2, 4, 256], BF16, name="g%d" % u, tag="g", bufs=3)
            nc.sync.dma_start(out=gt[u][:].rearrange("p b j t -> p b (j t)"), in_=unit_view(grad_out, u))

        RAW = [("w", 0), ("x", 0), ("x", 1), ("w", 1), ("x", 2), ("x", 3), ("w", 2), ("x", 4), ("x", 5), ("w", 3), ("x", 6), ("x", 7)]

        def load_raw(r):
            kind, n = RAW[r]
            raw[r] = sb.tile([P, 4, 512], BF16, name="raw%d" % r, tag="raw", bufs=5)
            if kind == "w":
                nc.sync.dma_start(out=raw[r][:], in_=wc[n].rearrange("(m t) k -> m t k", t=4))
            else:
                i, g = divmod(n, 2)
                for bb in range(2):
                    nc.sync.dma_start(
                        out=raw[r][:, :, 256 * bb : 256 * (bb + 1)],
                        in_=x[2 * g + bb, CD * i : CD * (i + 1)].rearrange("(p j) h w -> p j (h w)", j=4),
                    )

        def fill_bank(key, src, h, tag):
            words = src[:].rearrange("p j t -> p (j t)").bitcast(F32)
            banks[key] = psum.tile([P, 512], F32, name="tp_%s" % key, tag=tag, bufs=2)
            for jj in range(2):
                for w in range(2):
                    j = 2 * h + jj
                    c = 128 * (2 * jj + w)
                    nc.tensor.transpose(banks[key][:, c : c + 128], words[:, 256 * j + w : 256 * (j + 1) : 2], ident[:])

        def empty_bank(eng_copy, key, dst, h):
            out = dst[:].bitcast(F32)[:, 512 * h : 512 * (h + 1)].rearrange("q (j m w) -> q j m w", j=2, w=2)
            eng_copy(out=out, in_=banks[key][:].rearrange("q (j w m) -> q j m w", j=2, w=2))

        def new_grp(key):
            grp[key] = sb.tile([P, 2048], BF16, name="grp_%s" % key, tag="grp", bufs=2, align_bytes=64)

        def quant(codes, scales, key, tag, bufs, src, fmt):
            codes[key] = sb.tile([P, 512], U32, name="%s%s" % (tag, key), tag=tag, bufs=bufs, align_bytes=64)
            scales[key] = sb.tile([P, 512], U8, name="%ss%s" % (tag, key), tag=tag + "s", bufs=bufs, align_bytes=64)
            nc.vector.quantize_mx(out=codes[key][:].bitcast(fmt), scales=scales[key][:], in_=src)

        def sq(u):
            st[u] = sb.tile([P, 2, 4, 256], F32, name="s%d" % u, tag="s", bufs=4)
            nc.scalar.activation(out=flat(st[u]), in_=flat(zt[u]), func=AF.Square)

        def ln(u):
            lt[u] = sb.tile([P, 2, 4, 256], F32, name="l%d" % u, tag="l", bufs=3)
            nc.scalar.activation(out=flat(lt[u]), in_=flat(st[u]), func=AF.Ln)

        def ee(u):
            nc.scalar.activation(out=flat(st[u]), in_=flat(st[u]), func=AF.Exp, scale=-0.5)

        def rs(u):
            nc.scalar.activation(out=flat(lt[u]), in_=flat(lt[u]), func=AF.Exp, scale=-1.0)

        def ge(u):
            at[u] = sb.tile([P, 2, 4, 256], F32, name="a%d" % u, tag="a", bufs=5)
            if u == 0:
                for b in range(2):
                    nc.scalar.activation(out=flat(at[u])[:, 1024 * b : 1024 * (b + 1)], in_=flat(zt[u])[:, 1024 * b : 1024 * (b + 1)], func=AF.Gelu)
            else:
                nc.scalar.activation(out=flat(at[u]), in_=flat(zt[u]), func=AF.Gelu)

        def ev_t(u):
            new_grp("t%d" % u)
            for h in range(2):
                empty_bank(nc.scalar.copy if u + 1 >= LATE else nc.vector.tensor_copy, "t%d_%d" % (u, h), grp["t%d" % u], h)

        def ev_1(eng_copy, i, jj):
            o1s = sb.tile([P, 512], F32, name="o1s%d_%d" % (i, jj), tag="o1s", bufs=4)
            eng_copy(out=o1s[:].rearrange("q (m j) -> q m j", j=4), in_=o1[(i, jj)][:].rearrange("q (j m) -> q m j", j=4))
            nc.sync.dma_start(out=out_1[i].rearrange("(m t) k -> m t k", t=4)[:, jj, :], in_=o1s[:])

        def ev_1_act(half):
            for jj in (2 * (half % 2), 2 * (half % 2) + 1):
                ev_1(nc.scalar.copy, half // 2, jj)

        def sq_dve(u):
            st[u] = sb.tile([P, 2, 4, 256], F32, name="s%d" % u, tag="s", bufs=4)
            for c in ((0, 1024), (1024, 2048)) if u == 0 else ((0, 2048),):
                nc.vector.tensor_tensor(out=flat(st[u])[:, c[0] : c[1]], in0=flat(zt[u])[:, c[0] : c[1]], in1=flat(zt[u])[:, c[0] : c[1]], op=ALU.mult)

        def gp(u):
            eng = nc.gpsimd if u in POOL_GP else nc.vector
            eng.tensor_tensor(out=flat(zt[u]), in0=flat(zt[u]), in1=flat(gt[u]), op=ALU.mult)

        def k1(u):
            nc.vector.tensor_tensor(out=flat(at[u]), in0=flat(at[u]), in1=flat(lt[u]), op=ALU.mult)

        def k2(u):
            nc.vector.scalar_tensor_tensor(out=flat(at[u]), in0=flat(st[u]), scalar=INV_SQRT_2PI, in1=flat(at[u]), op0=ALU.mult, op1=ALU.add)

        def dz(u):
            eng = nc.vector if u >= LATE else nc.gpsimd
            eng.tensor_tensor(out=flat(at[u]), in0=flat(at[u]), in1=flat(zt[u]), op=ALU.mult)

        def castn(u):
            dzb[u] = sb.tile([P, 4, 512], BF16, name="dzb%d" % u, tag="dzb", bufs=2)
            eng_copy = nc.scalar.copy if u in (LATE - 1, LATE) else nc.vector.tensor_copy
            eng_copy(out=dzb[u][:].rearrange("p j (b t) -> p b j t", b=2), in_=at[u][:])

        def casti(u):
            gk[u] = sb.tile([P, 512, 4], BF16, name="gk%d" % u, tag="gk", bufs=1, align_bytes=64)
            eng_copy = nc.scalar.copy if u >= LATE else nc.vector.tensor_copy
            for b in range(2):
                eng_copy(
                    out=gk[u][:, 256 * b : 256 * (b + 1), :].rearrange("p (c i) j -> p c j i", i=4),
                    in_=at[u][:, b, :, :].rearrange("p j (c i) -> p c j i", i=4),
                )

        def qk(u):
            quant(kq, ks, u, "kq", 2, gk[u][:].rearrange("p t j -> p (t j)"), E5)

        def qt(u):
            quant(tq, ts, u, "tq", 4, grp["t%d" % u][:], E5)

        def res(u, t):
            nc.vector.tensor_tensor(out=at[u][:, :, t, :], in0=o0[(u, t)][:].rearrange("p (b t) -> p b t", b=2), in1=at[u][:, :, t, :], op=ALU.add)

        def store0(u):
            nc.sync.dma_start(out=unit_view(out_0, u), in_=at[u][:].rearrange("p b j t -> p b (j t)"))

        def tp_t(u):
            for h in range(2):
                fill_bank("t%d_%d" % (u, h), dzb[u], h, "tp")

        def mm0(u, t):
            i = u // 2
            o0[(u, t)] = psum.tile([P, 512], F32, name="o0_%d_%d" % (u, t), tag="o0", bufs=2)
            c = slice(128 * t, 128 * (t + 1))
            nc.tensor.matmul_mx(out=o0[(u, t)][:], lhsT=wq[i][:, c].bitcast(E4), lhsT_scale=ws[i][:, c], rhs=kq[u][:].bitcast(E5), rhs_scale=ks[u][:], start=True, stop=True)

        def mm1(half, tag):
            i = half // 2
            for jj in (2 * (half % 2), 2 * (half % 2) + 1):
                o1[(i, jj)] = psum.tile([P, 512], F32, name="o1_%d_%d" % (i, jj), tag=tag, bufs=2)
                c = slice(128 * jj, 128 * (jj + 1))
                for g in range(2):
                    u = 2 * i + g
                    nc.tensor.matmul_mx(out=o1[(i, jj)][:], lhsT=xq[u][:, c].bitcast(E4), lhsT_scale=xs[u][:, c], rhs=tq[u][:].bitcast(E5), rhs_scale=ts[u][:], start=(g == 0), stop=(g == 1))

        ident = const.tile([P, P], F32, name="ident")
        make_identity(nc, ident[:])
        warm = const.tile([P, 1], F32, name="warm")
        nc.vector.memset(warm[:], 1.0)
        nc.scalar.activation(out=warm[:], in_=warm[:], func=AF.Gelu)

        def raw_fill(r, h):
            fill_bank("r%d_%d" % (r, h), raw[r], h, "tr")

        def raw_empty(r, h):
            if h == 0:
                new_grp("r%d" % r)
            empty_bank(nc.vector.tensor_copy, "r%d_%d" % (r, h), grp["r%d" % r], h)

        def raw_quant(r):
            kind, n = RAW[r]
            if kind == "w":
                quant(wq, ws, n, "wq", 4, grp["r%d" % r][:], E4)
            else:
                quant(xq, xs, n, "xq", 8, grp["r%d" % r][:], E4)

        load_z(0)
        load_z(1)
        for r in range(3):
            load_raw(r)
        load_g(0)
        for r in range(3, 5):
            load_raw(r)

        def act_half(n):
            v = n // 2 + 1
            if 2 * v >= UNITS:
                return
            if n % 2 == 0:
                if n == 0:
                    ge(1)
                ge(2 * v)
                ge(2 * v + 1)
                sq(2 * v)
                sq(2 * v + 1)
                ln(2 * v)
            else:
                ln(2 * v + 1)
                for u in (2 * v, 2 * v + 1):
                    ee(u)
                    rs(u)

        ge(0)
        sq_dve(0)
        sq_dve(1)
        ln(0)
        ln(1)
        for u in (0, 1):
            ee(u)
            rs(u)
        for u in POOL_GP:
            gp(u)

        late_loads = {3: (load_z, 2), 5: (load_z, 3), 7: (load_g, 1)}
        nb = 2 * HEAD_RAWS
        for k in range(nb + 3):
            if k < nb:
                raw_fill(k // 2, k % 2)
                if k % 2 == 1 and k // 2 + 5 < len(RAW):
                    load_raw(k // 2 + 5)
                if k in late_loads:
                    late_loads[k][0](late_loads[k][1])
            if 1 <= k <= nb:
                raw_empty((k - 1) // 2, (k - 1) % 2)
            if k >= 3 and k % 2 == 1:
                raw_quant((k - 3) // 2)

        gp(0)
        step_raws = {0: (5, 6, 7), 1: (8,), 2: (9,), 3: (10,), 4: (11,)}

        for n in range(UNITS + 1):
            cur = n < UNITS
            old = n >= 1
            late = n >= LATE
            raws = step_raws.get(n, ())
            if n == LATE:
                castn(n - 1)
                tp_t(n - 1)
            if 3 <= n and n != LATE - 1:
                ev_1_act(n - 3)
            if late:
                ev_t(n - 1)
            act_half(n)
            if raws:
                raw_fill(raws[0], 0)
                raw_fill(raws[0], 1)
            if cur:
                k1(n)
                if n > 0:
                    gp(n)
                k2(n)
                dz(n)
            if cur and late:
                if n == UNITS - 1:
                    castn(n)
                casti(n)
                if n < UNITS - 1:
                    castn(n)
            if old:
                res(n - 1, 0)
                res(n - 1, 1)
                mm0(n - 1, 2)
                mm0(n - 1, 3)
                if not late:
                    ev_t(n - 1)
                res(n - 1, 2)
                res(n - 1, 3)
                store0(n - 1)
            if n == LATE - 1:
                for jj in (0, 1):
                    ev_1(nc.vector.tensor_copy, (n - 3) // 2, 2 * ((n - 3) % 2) + jj)
            for q in range(len(raws)):
                for h in range(2):
                    raw_empty(raws[q], h)
                    if q + 1 < len(raws):
                        raw_fill(raws[q + 1], h)
                if raws[q] + 5 < len(RAW):
                    load_raw(raws[q] + 5)
                if q + 1 < len(raws):
                    raw_quant(raws[q])
            if cur and n < LATE - 1:
                castn(n)
                tp_t(n)
            if old:
                qt(n - 1)
            if n >= 2:
                mm1(n - 2, "o1")
            if n == UNITS:
                mm1(n - 1, "tr")
            if cur and not late:
                casti(n)
            if raws:
                raw_quant(raws[-1])
            if cur:
                qk(n)
                mm0(n, 0)
                mm0(n, 1)
            if cur and late:
                tp_t(n)
            if n + 4 < UNITS:
                load_z(n + 4)
            if n + 2 < UNITS:
                load_g(n + 2)
        ev_1(nc.scalar.copy, 3, 0)
        ev_1(nc.vector.tensor_copy, 3, 1)
        ev_1(nc.scalar.copy, 3, 2)
        ev_1(nc.vector.tensor_copy, 3, 3)
